import numpy as np
import ml_dtypes

BF16 = ml_dtypes.bfloat16


def bf(x):
    return np.asarray(x, np.float32).astype(BF16)


def f32(x):
    return np.asarray(x, np.float32)


def f64(x):
    return np.asarray(x).astype(np.float64)


def striped(idx):
    return np.tile(idx.reshape(-1, 16).T, (8, 1))


D, S, H, SP, O, N = 128, 256, 512, 128, 256, 256
ALPHA, BETA = 5.0, 0.5


def sigmoid(v):
    return 1.0 / (1.0 + np.exp(-v))


def setup_inputs():
    tok = 0.5 + np.random.rand(1, S)
    table = bf(np.random.standard_normal((D, S)) * tok)
    w = bf(0.25 * np.random.standard_normal((D, H)) / np.sqrt(D))
    w_out = f32(0.1 * np.random.standard_normal((O, SP)))
    return {"table": table, "w": w, "w_out": w_out, "offs": striped(np.random.permutation(S)[:N])}


def reference(table, w, w_out, offs):
    idx = offs[:16].T.reshape(-1)
    z = f64(w).T @ f64(table)[:, idx]
    p = sigmoid(ALPHA * (z - BETA))
    norm = p.sum(axis=0, keepdims=True) / SP
    return f64(w_out).sum(axis=1, keepdims=True) * norm

@@ -1,0 +1,53 @@
+import concourse.mybir as mybir
+
+BF16, F32, U16 = mybir.dt.bfloat16, mybir.dt.float32, mybir.dt.uint16
+SIGMOID = mybir.ActivationFunctionType.Sigmoid
+
+P = 128
+D, S, H, SP, O, N = 128, 256, 512, 128, 256, 256
+ALPHA, BETA = 5.0, 0.5
+H_BLOCKS = H // P
+O_BLOCKS = O // P
+
+assert D == P and SP & (SP - 1) == 0
+
+FLOPS = 2 * D * H * N + 2 * H * N + O * SP + O * N
+
+
+def tile_sparsemlp_kernel(tc, table, w, w_out, offs, out):
+    nc = tc.nc
+    with (
+        tc.tile_pool(name="held", bufs=1) as held,
+        tc.psum_pool(name="psum", bufs=1) as psum,
+    ):
+        offsets = held.tile([P, N // 16], U16, name="offsets")
+        nc.sync.dma_start(offsets[:], offs)
+        tokens = held.tile([P, S], BF16, name="tokens")
+        nc.sync.dma_start(tokens[:], table)
+        weights = held.tile([P, H], BF16, name="weights")
+        nc.scalar.dma_start(weights[:], w)
+        selected = held.tile([P, O_BLOCKS, SP], F32, name="selected")
+        nc.gpsimd.dma_start(selected[:], w_out.rearrange("(b p) s -> p b s", p=P))
+
+        shift = held.tile([P, 1], F32, name="shift")
+        nc.vector.memset(shift[:], -ALPHA * BETA)
+        averager = held.tile([P, P], BF16, name="averager")
+        nc.vector.memset(averager[:], 1.0 / SP)
+
+        gain = held.tile([P, O_BLOCKS], F32, name="gain")
+        nc.vector.reduce_sum(gain[:], selected[:], axis=mybir.AxisListType.X)
+
+        norm = psum.tile([P, N], F32, name="norm")
+        for b in range(H_BLOCKS):
+            z = psum.tile([P, N], F32, name=f"z{b}")
+            nc.tensor.matmul(
+                z[:], weights[:, b * P : (b + 1) * P], tokens[:].indirect(offsets[:]), start=True, stop=True
+            )
+            p = held.tile([P, N], BF16, name=f"p{b}")
+            nc.scalar.activation(p[:], z[:], SIGMOID, bias=shift[:], scale=ALPHA)
+            nc.tensor.matmul(norm[:], averager[:], p[:], start=(b == 0), stop=(b == H_BLOCKS - 1))
+
+        for b in range(O_BLOCKS):
+            scaled = held.tile([P, N], F32, name=f"scaled{b}")
+            nc.vector.tensor_scalar_mul(scaled[:], norm[:], gain[:, b : b + 1])
+            nc.sync.dma_start(out[b * P : (b + 1) * P, :], scaled[:])

@@ -37,14 +37,16 @@ def tile_sparsemlp_kernel(tc, table, w, w_out, offs, out):
         gain = held.tile([P, O_BLOCKS], F32, name="gain")
         nc.vector.reduce_sum(gain[:], selected[:], axis=mybir.AxisListType.X)
 
+        z = [psum.tile([P, N], F32, name=f"z{b}") for b in range(H_BLOCKS)]
+        for b in range(H_BLOCKS):
+            nc.tensor.matmul(
+                z[b][:], weights[:, b * P : (b + 1) * P], tokens[:].indirect(offsets[:]), start=True, stop=True
+            )
+
         norm = psum.tile([P, N], F32, name="norm")
         for b in range(H_BLOCKS):
-            z = psum.tile([P, N], F32, name=f"z{b}")
-            nc.tensor.matmul(
-                z[:], weights[:, b * P : (b + 1) * P], tokens[:].indirect(offsets[:]), start=True, stop=True
-            )
             p = held.tile([P, N], BF16, name=f"p{b}")
-            nc.scalar.activation(p[:], z[:], SIGMOID, bias=shift[:], scale=ALPHA)
+            nc.scalar.activation(p[:], z[b][:], SIGMOID, bias=shift[:], scale=ALPHA)
             nc.tensor.matmul(norm[:], averager[:], p[:], start=(b == 0), stop=(b == H_BLOCKS - 1))
 
         for b in range(O_BLOCKS):

@@ -8,6 +8,9 @@ D, S, H, SP, O, N = 128, 256, 512, 128, 256, 256
 ALPHA, BETA = 5.0, 0.5
 H_BLOCKS = H // P
 O_BLOCKS = O // P
+HALVES = 2
+NH = N // HALVES
+PAIR = 2
 
 assert D == P and SP & (SP - 1) == 0
 
@@ -37,19 +40,28 @@ def tile_sparsemlp_kernel(tc, table, w, w_out, offs, out):
         gain = held.tile([P, O_BLOCKS], F32, name="gain")
         nc.vector.reduce_sum(gain[:], selected[:], axis=mybir.AxisListType.X)
 
-        z = [psum.tile([P, N], F32, name=f"z{b}") for b in range(H_BLOCKS)]
-        for b in range(H_BLOCKS):
-            nc.tensor.matmul(
-                z[b][:], weights[:, b * P : (b + 1) * P], tokens[:].indirect(offsets[:]), start=True, stop=True
-            )
+        z = {}
+        for c in range(HALVES):
+            picked = tokens[:].indirect(offsets[:, c * NH // 16 : (c + 1) * NH // 16])
+            for q in range(H_BLOCKS // PAIR):
+                z[c, q] = psum.tile([P, PAIR * NH], F32, name=f"z{c}{q}")
+                for k in range(PAIR):
+                    b = q * PAIR + k
+                    nc.tensor.matmul(
+                        z[c, q][:, k * NH : (k + 1) * NH], weights[:, b * P : (b + 1) * P], picked, start=True, stop=True
+                    )
 
-        norm = psum.tile([P, N], F32, name="norm")
-        for b in range(H_BLOCKS):
-            p = held.tile([P, N], BF16, name=f"p{b}")
-            nc.scalar.activation(p[:], z[b][:], SIGMOID, bias=shift[:], scale=ALPHA)
-            nc.tensor.matmul(norm[:], averager[:], p[:], start=(b == 0), stop=(b == H_BLOCKS - 1))
-
-        for b in range(O_BLOCKS):
-            scaled = held.tile([P, N], F32, name=f"scaled{b}")
-            nc.vector.tensor_scalar_mul(scaled[:], norm[:], gain[:, b : b + 1])
-            nc.sync.dma_start(out[b * P : (b + 1) * P, :], scaled[:])
+        for c in range(HALVES):
+            norm = psum.tile([P, NH], F32, name=f"norm{c}")
+            for q in range(H_BLOCKS // PAIR):
+                p = held.tile([P, PAIR * NH], BF16, name=f"p{c}{q}")
+                nc.scalar.activation(p[:], z[c, q][:], SIGMOID, bias=shift[:], scale=ALPHA)
+                for k in range(PAIR):
+                    b = q * PAIR + k
+                    nc.tensor.matmul(
+                        norm[:], averager[:], p[:, k * NH : (k + 1) * NH], start=(b == 0), stop=(b == H_BLOCKS - 1)
+                    )
+            for b in range(O_BLOCKS):
+                scaled = held.tile([P, NH], F32, name=f"scaled{c}{b}")
+                nc.vector.tensor_scalar_mul(scaled[:], norm[:], gain[:, b : b + 1])
+                nc.sync.dma_start(out[b * P : (b + 1) * P, c * NH : (c + 1) * NH], scaled[:])

@@ -11,6 +11,8 @@ O_BLOCKS = O // P
 HALVES = 2
 NH = N // HALVES
 PAIR = 2
+BANK = 512
+WARM_UP = 3
 
 assert D == P and SP & (SP - 1) == 0
 
@@ -27,10 +29,17 @@ def tile_sparsemlp_kernel(tc, table, w, w_out, offs, out):
         nc.sync.dma_start(offsets[:], offs)
         tokens = held.tile([P, S], BF16, name="tokens")
         nc.sync.dma_start(tokens[:], table)
-        weights = held.tile([P, H], BF16, name="weights")
-        nc.scalar.dma_start(weights[:], w)
+        weights = [held.tile([P, PAIR * P], BF16, name=f"weights{q}") for q in range(H_BLOCKS // PAIR)]
+        for q in range(H_BLOCKS // PAIR):
+            nc.scalar.dma_start(weights[q][:], w[:, q * PAIR * P : (q + 1) * PAIR * P])
         selected = held.tile([P, O_BLOCKS, SP], F32, name="selected")
         nc.gpsimd.dma_start(selected[:], w_out.rearrange("(b p) s -> p b s", p=P))
+
+        zeros = held.tile([P, BANK], BF16, name="zeros")
+        nc.vector.memset(zeros[:], 0.0)
+        unread = psum.tile([P, BANK], F32, name="unread")
+        for i in range(WARM_UP):
+            nc.tensor.matmul(unread[:], zeros[:, 0:P], zeros[:], start=True, stop=True)
 
         shift = held.tile([P, 1], F32, name="shift")
         nc.vector.memset(shift[:], -ALPHA * BETA)
@@ -46,9 +55,8 @@ def tile_sparsemlp_kernel(tc, table, w, w_out, offs, out):
             for q in range(H_BLOCKS // PAIR):
                 z[c, q] = psum.tile([P, PAIR * NH], F32, name=f"z{c}{q}")
                 for k in range(PAIR):
-                    b = q * PAIR + k
                     nc.tensor.matmul(
-                        z[c, q][:, k * NH : (k + 1) * NH], weights[:, b * P : (b + 1) * P], picked, start=True, stop=True
+                        z[c, q][:, k * NH : (k + 1) * NH], weights[q][:, k * P : (k + 1) * P], picked, start=True, stop=True
                     )
 
         for c in range(HALVES):

@@ -11,6 +11,8 @@ O_BLOCKS = O // P
 HALVES = 2
 NH = N // HALVES
 PAIR = 2
+SIDE_BY_SIDE = (2, 1)
+PSUM_BANKS = 8
 BANK = 512
 WARM_UP = 3
 
@@ -23,12 +25,12 @@ def tile_sparsemlp_kernel(tc, table, w, w_out, offs, out):
     nc = tc.nc
     with (
         tc.tile_pool(name="held", bufs=1) as held,
-        tc.psum_pool(name="psum", bufs=1) as psum,
+        tc.psum_pool(name="psum", bufs=PSUM_BANKS) as psum,
     ):
-        offsets = held.tile([P, N // 16], U16, name="offsets")
-        nc.sync.dma_start(offsets[:], offs)
         tokens = held.tile([P, S], BF16, name="tokens")
         nc.sync.dma_start(tokens[:], table)
+        offsets = held.tile([P, N // 16], U16, name="offsets")
+        nc.sync.dma_start(offsets[:], offs)
         weights = [held.tile([P, PAIR * P], BF16, name=f"weights{q}") for q in range(H_BLOCKS // PAIR)]
         for q in range(H_BLOCKS // PAIR):
             nc.scalar.dma_start(weights[q][:], w[:, q * PAIR * P : (q + 1) * PAIR * P])
@@ -37,7 +39,7 @@ def tile_sparsemlp_kernel(tc, table, w, w_out, offs, out):
 
         zeros = held.tile([P, BANK], BF16, name="zeros")
         nc.vector.memset(zeros[:], 0.0)
-        unread = psum.tile([P, BANK], F32, name="unread")
+        unread = psum.tile([P, BANK], F32, name="unread", tag="bank")
         for i in range(WARM_UP):
             nc.tensor.matmul(unread[:], zeros[:, 0:P], zeros[:], start=True, stop=True)
 
@@ -52,20 +54,25 @@ def tile_sparsemlp_kernel(tc, table, w, w_out, offs, out):
         z = {}
         for c in range(HALVES):
             picked = tokens[:].indirect(offsets[:, c * NH // 16 : (c + 1) * NH // 16])
-            for q in range(H_BLOCKS // PAIR):
-                z[c, q] = psum.tile([P, PAIR * NH], F32, name=f"z{c}{q}")
-                for k in range(PAIR):
-                    nc.tensor.matmul(
-                        z[c, q][:, k * NH : (k + 1) * NH], weights[q][:, k * P : (k + 1) * P], picked, start=True, stop=True
-                    )
+            for b in range(H_BLOCKS):
+                q, k = divmod(b, SIDE_BY_SIDE[c])
+                if k == 0:
+                    z[c, q] = psum.tile([P, SIDE_BY_SIDE[c] * NH], F32, name=f"z{c}{q}", tag="bank")
+                nc.tensor.matmul(
+                    z[c, q][:, k * NH : (k + 1) * NH],
+                    weights[b // PAIR][:, (b % PAIR) * P : (b % PAIR + 1) * P],
+                    picked,
+                    start=True,
+                    stop=True,
+                )
 
         for c in range(HALVES):
-            norm = psum.tile([P, NH], F32, name=f"norm{c}")
-            for q in range(H_BLOCKS // PAIR):
-                p = held.tile([P, PAIR * NH], BF16, name=f"p{c}{q}")
+            norm = psum.tile([P, NH], F32, name=f"norm{c}", tag="bank")
+            for q in range(H_BLOCKS // SIDE_BY_SIDE[c]):
+                p = held.tile([P, SIDE_BY_SIDE[c] * NH], BF16, name=f"p{c}{q}")
                 nc.scalar.activation(p[:], z[c, q][:], SIGMOID, bias=shift[:], scale=ALPHA)
-                for k in range(PAIR):
-                    b = q * PAIR + k
+                for k in range(SIDE_BY_SIDE[c]):
+                    b = q * SIDE_BY_SIDE[c] + k
                     nc.tensor.matmul(
                         norm[:], averager[:], p[:, k * NH : (k + 1) * NH], start=(b == 0), stop=(b == H_BLOCKS - 1)
                     )

@@ -35,7 +35,7 @@ def tile_sparsemlp_kernel(tc, table, w, w_out, offs, out):
         for q in range(H_BLOCKS // PAIR):
             nc.scalar.dma_start(weights[q][:], w[:, q * PAIR * P : (q + 1) * PAIR * P])
         selected = held.tile([P, O_BLOCKS, SP], F32, name="selected")
-        nc.gpsimd.dma_start(selected[:], w_out.rearrange("(b p) s -> p b s", p=P))
+        nc.sync.dma_start(selected[:], w_out.rearrange("(b p) s -> p b s", p=P))
 
         zeros = held.tile([P, BANK], BF16, name="zeros")
         nc.vector.memset(zeros[:], 0.0)

@@ -37,16 +37,15 @@ def tile_sparsemlp_kernel(tc, table, w, w_out, offs, out):
         selected = held.tile([P, O_BLOCKS, SP], F32, name="selected")
         nc.sync.dma_start(selected[:], w_out.rearrange("(b p) s -> p b s", p=P))
 
-        zeros = held.tile([P, BANK], BF16, name="zeros")
-        nc.vector.memset(zeros[:], 0.0)
-        unread = psum.tile([P, BANK], F32, name="unread", tag="bank")
+        averager = held.tile([P, P], BF16, name="averager")
+        nc.vector.memset(averager[:], 1.0 / SP)
+        unread = psum.tile([P, BANK // P, P], F32, name="unread", tag="bank")
         for i in range(WARM_UP):
-            nc.tensor.matmul(unread[:], zeros[:, 0:P], zeros[:], start=True, stop=True)
+            repeated = averager[:].unsqueeze(1).to_broadcast([P, BANK // P, P])
+            nc.tensor.matmul(unread[:], averager[:], repeated, start=True, stop=True)
 
         shift = held.tile([P, 1], F32, name="shift")
         nc.vector.memset(shift[:], -ALPHA * BETA)
-        averager = held.tile([P, P], BF16, name="averager")
-        nc.vector.memset(averager[:], 1.0 / SP)
 
         gain = held.tile([P, O_BLOCKS], F32, name="gain")
         nc.vector.reduce_sum(gain[:], selected[:], axis=mybir.AxisListType.X)

@@ -65,6 +65,7 @@ def tile_sparsemlp_kernel(tc, table, w, w_out, offs, out):
                     stop=True,
                 )
 
+        scaled = [held.tile([P, N], F32, name=f"scaled{b}") for b in range(O_BLOCKS)]
         for c in range(HALVES):
             norm = psum.tile([P, NH], F32, name=f"norm{c}", tag="bank")
             for q in range(H_BLOCKS // SIDE_BY_SIDE[c]):
@@ -76,6 +77,6 @@ def tile_sparsemlp_kernel(tc, table, w, w_out, offs, out):
                         norm[:], averager[:], p[:, k * NH : (k + 1) * NH], start=(b == 0), stop=(b == H_BLOCKS - 1)
                     )
             for b in range(O_BLOCKS):
-                scaled = held.tile([P, NH], F32, name=f"scaled{c}{b}")
-                nc.vector.tensor_scalar_mul(scaled[:], norm[:], gain[:, b : b + 1])
-                nc.sync.dma_start(out[b * P : (b + 1) * P, c * NH : (c + 1) * NH], scaled[:])
+                nc.vector.tensor_scalar_mul(scaled[b][:, c * NH : (c + 1) * NH], norm[:], gain[:, b : b + 1])
+        for b in range(O_BLOCKS):
+            nc.sync.dma_start(out[b * P : (b + 1) * P, :], scaled[b][:])

@@ -10,7 +10,6 @@ H_BLOCKS = H // P
 O_BLOCKS = O // P
 HALVES = 2
 NH = N // HALVES
-PAIR = 2
 SIDE_BY_SIDE = (2, 1)
 PSUM_BANKS = 8
 BANK = 512
@@ -31,9 +30,9 @@ def tile_sparsemlp_kernel(tc, table, w, w_out, offs, out):
         nc.sync.dma_start(tokens[:], table)
         offsets = held.tile([P, N // 16], U16, name="offsets")
         nc.sync.dma_start(offsets[:], offs)
-        weights = [held.tile([P, PAIR * P], BF16, name=f"weights{q}") for q in range(H_BLOCKS // PAIR)]
-        for q in range(H_BLOCKS // PAIR):
-            nc.scalar.dma_start(weights[q][:], w[:, q * PAIR * P : (q + 1) * PAIR * P])
+        weights = held.tile([P, H], BF16, name="weights")
+        for queue, first, last in ((nc.scalar, 0, 1), (nc.scalar, 1, 2), (nc.sync, 2, H_BLOCKS)):
+            queue.dma_start(weights[:, first * P : last * P], w[:, first * P : last * P])
         selected = held.tile([P, O_BLOCKS, SP], F32, name="selected")
         nc.sync.dma_start(selected[:], w_out.rearrange("(b p) s -> p b s", p=P))
 
@@ -59,7 +58,7 @@ def tile_sparsemlp_kernel(tc, table, w, w_out, offs, out):
                     z[c, q] = psum.tile([P, SIDE_BY_SIDE[c] * NH], F32, name=f"z{c}{q}", tag="bank")
                 nc.tensor.matmul(
                     z[c, q][:, k * NH : (k + 1) * NH],
-                    weights[b // PAIR][:, (b % PAIR) * P : (b % PAIR + 1) * P],
+                    weights[:, b * P : (b + 1) * P],
                     picked,
                     start=True,
                     stop=True,

@@ -34,7 +34,7 @@ def tile_sparsemlp_kernel(tc, table, w, w_out, offs, out):
         for queue, first, last in ((nc.scalar, 0, 1), (nc.scalar, 1, 2), (nc.sync, 2, H_BLOCKS)):
             queue.dma_start(weights[:, first * P : last * P], w[:, first * P : last * P])
         selected = held.tile([P, O_BLOCKS, SP], F32, name="selected")
-        nc.sync.dma_start(selected[:], w_out.rearrange("(b p) s -> p b s", p=P))
+        nc.sync.dma_start(selected[:], w_out.rearrange("(p b) s -> p b s", p=P))
 
         averager = held.tile([P, P], BF16, name="averager")
         nc.vector.memset(averager[:], 1.0 / SP)
@@ -77,5 +77,6 @@ def tile_sparsemlp_kernel(tc, table, w, w_out, offs, out):
                     )
             for b in range(O_BLOCKS):
                 nc.vector.tensor_scalar_mul(scaled[b][:, c * NH : (c + 1) * NH], norm[:], gain[:, b : b + 1])
+        rows = out.rearrange("(p b) j -> p b j", p=P)
         for b in range(O_BLOCKS):
-            nc.sync.dma_start(out[b * P : (b + 1) * P, :], scaled[b][:])
+            nc.sync.dma_start(rows[:, b, :], scaled[b][:])

import concourse.mybir as mybir

BF16, F32, U16 = mybir.dt.bfloat16, mybir.dt.float32, mybir.dt.uint16
SIGMOID = mybir.ActivationFunctionType.Sigmoid

P = 128
D, S, H, SP, O, N = 128, 256, 512, 128, 256, 256
ALPHA, BETA = 5.0, 0.5
H_BLOCKS = H // P
O_BLOCKS = O // P
HALVES = 2
NH = N // HALVES
SIDE_BY_SIDE = (2, 1)
PSUM_BANKS = 8
BANK = 512
WARM_UP = 3

assert D == P and SP & (SP - 1) == 0

FLOPS = 2 * D * H * N + 2 * H * N + O * SP + O * N


def tile_sparsemlp_kernel(tc, table, w, w_out, offs, out):
    nc = tc.nc
    with (
        tc.tile_pool(name="held", bufs=1) as held,
        tc.psum_pool(name="psum", bufs=PSUM_BANKS) as psum,
    ):
        tokens = held.tile([P, S], BF16, name="tokens")
        nc.sync.dma_start(tokens[:], table)
        offsets = held.tile([P, N // 16], U16, name="offsets")
        nc.sync.dma_start(offsets[:], offs)
        weights = held.tile([P, H], BF16, name="weights")
        for queue, first, last in ((nc.scalar, 0, 1), (nc.scalar, 1, 2), (nc.sync, 2, H_BLOCKS)):
            queue.dma_start(weights[:, first * P : last * P], w[:, first * P : last * P])
        selected = held.tile([P, O_BLOCKS, SP], F32, name="selected")
        nc.sync.dma_start(selected[:], w_out.rearrange("(p b) s -> p b s", p=P))

        averager = held.tile([P, P], BF16, name="averager")
        nc.vector.memset(averager[:], 1.0 / SP)
        unread = psum.tile([P, BANK // P, P], F32, name="unread", tag="bank")
        for i in range(WARM_UP):
            repeated = averager[:].unsqueeze(1).to_broadcast([P, BANK // P, P])
            nc.tensor.matmul(unread[:], averager[:], repeated, start=True, stop=True)

        shift = held.tile([P, 1], F32, name="shift")
        nc.vector.memset(shift[:], -ALPHA * BETA)

        gain = held.tile([P, O_BLOCKS], F32, name="gain")
        nc.vector.reduce_sum(gain[:], selected[:], axis=mybir.AxisListType.X)

        z = {}
        for c in range(HALVES):
            picked = tokens[:].indirect(offsets[:, c * NH // 16 : (c + 1) * NH // 16])
            for b in range(H_BLOCKS):
                q, k = divmod(b, SIDE_BY_SIDE[c])
                if k == 0:
                    z[c, q] = psum.tile([P, SIDE_BY_SIDE[c] * NH], F32, name=f"z{c}{q}", tag="bank")
                nc.tensor.matmul(
                    z[c, q][:, k * NH : (k + 1) * NH],
                    weights[:, b * P : (b + 1) * P],
                    picked,
                    start=True,
                    stop=True,
                )

        scaled = [held.tile([P, N], F32, name=f"scaled{b}") for b in range(O_BLOCKS)]
        for c in range(HALVES):
            norm = psum.tile([P, NH], F32, name=f"norm{c}", tag="bank")
            for q in range(H_BLOCKS // SIDE_BY_SIDE[c]):
                p = held.tile([P, SIDE_BY_SIDE[c] * NH], BF16, name=f"p{c}{q}")
                nc.scalar.activation(p[:], z[c, q][:], SIGMOID, bias=shift[:], scale=ALPHA)
                for k in range(SIDE_BY_SIDE[c]):
                    b = q * SIDE_BY_SIDE[c] + k
                    nc.tensor.matmul(
                        norm[:], averager[:], p[:, k * NH : (k + 1) * NH], start=(b == 0), stop=(b == H_BLOCKS - 1)
                    )
            for b in range(O_BLOCKS):
                nc.vector.tensor_scalar_mul(scaled[b][:, c * NH : (c + 1) * NH], norm[:], gain[:, b : b + 1])
        rows = out.rearrange("(p b) j -> p b j", p=P)
        for b in range(O_BLOCKS):
            nc.sync.dma_start(rows[:, b, :], scaled[b][:])
